import numpy as np
import ml_dtypes


def mxq(x, axis, fmt="e4m3"):
    dtype, down = {"e4m3": (ml_dtypes.float8_e4m3fn, 7), "e5m2": (ml_dtypes.float8_e5m2, 14)}[fmt]
    v = np.moveaxis(np.asarray(x, np.float32).astype(ml_dtypes.bfloat16).astype(np.float64), axis, -1)
    blocks = v.reshape(v.shape[:-1] + (-1, 32))
    amax = np.abs(blocks).max(-1, keepdims=True)
    byte = np.maximum(np.where(amax > 0, np.frexp(amax)[1] - 1 + 127, 0) - down, 1)
    scale = np.exp2(byte - 127.0)
    codes = (blocks / scale).astype(np.float32).astype(dtype).astype(np.float64)
    return np.moveaxis((codes * scale).reshape(v.shape), -1, axis)


WIDE = False


def mx_kscale(k):
    if not WIDE:
        return np.ones(k)
    levels = np.array([10, -10, 5, -5, 0])
    a = np.random.permutation(np.resize(levels, k // 512 * 4)).reshape(k // 512, 4)
    idx = np.arange(k)
    return np.exp2(a[idx // 512, idx % 128 // 32])


BF16 = ml_dtypes.bfloat16


def bf(x):
    return np.asarray(x, np.float32).astype(BF16)


def f64(x):
    return np.asarray(x).astype(np.float64)


B, H, O, I, K = 128, 512, 32, 32, 512


def silu(v):
    return v / (1.0 + np.exp(-v))


def setup_inputs():
    s = mx_kscale(H)
    return {
        "hk": bf(silu(np.random.standard_normal((B, H))) * s),
        "kw2": bf(np.random.standard_normal((H, K)) * 1.5 / np.sqrt(H) / s[:, None]),
        "kb2": bf(np.random.standard_normal(K) * 0.3),
        "bases": bf(np.random.standard_normal((K, O, I)) * 1.5 / np.sqrt(K)),
        "base": bf(np.random.standard_normal((O, I)) * 0.7),
        "row": bf(1.0 + 0.1 * np.tanh(np.random.standard_normal((B, O)))),
        "col": bf(1.0 + 0.1 * np.tanh(np.random.standard_normal((B, I)))),
    }


def reference(hk, kw2, kb2, bases, base, row, col):
    coeff = np.tanh((mxq(f64(hk), 1, "e4m3") @ mxq(f64(kw2), 0, "e4m3")) + f64(kb2))
    delta = (mxq(coeff, 1, "e4m3") @ mxq(f64(bases).reshape(K, O * I), 0, "e4m3")).reshape(B, O, I)
    weight = (f64(base)[None] + delta) * f64(row)[:, :, None] * f64(col)[:, None, :]
    return weight, coeff

@@ -1,0 +1,175 @@
+from contextlib import ExitStack
+
+import concourse.mybir as mybir
+from concourse.masks import make_identity
+
+F32 = mybir.dt.float32
+BF16 = mybir.dt.bfloat16
+U32 = mybir.dt.uint32
+U8 = mybir.dt.uint8
+FP8X4 = mybir.dt.float8_e4m3fn_x4
+ADD = mybir.AluOpType.add
+MULT = mybir.AluOpType.mult
+TANH = mybir.ActivationFunctionType.Tanh
+
+P = 128
+PACK = 4
+B, H, K, O, I = 128, 512, 512, 32, 32
+OI = O * I
+N_TILE = 512
+N_TILES = OI // N_TILE
+RUN = 4
+
+FLOPS = 2 * B * H * K + 2 * B * K * OI
+
+
+def regroup(engine_copy, grouped, raw, cols):
+    engine_copy(
+        out=grouped[:, cols, :].rearrange("p (c i) j -> p c j i", i=RUN),
+        in_=raw[:, :, cols].rearrange("p j (c i) -> p c j i", i=RUN),
+    )
+
+
+def tile_structuredternaryfactorgenerator_pa_s_kernel(
+    tc, hk, kw2, kb2, bases, base, row, col, weight, coeff
+):
+    nc = tc.nc
+    with ExitStack() as ctx:
+        keep = ctx.enter_context(tc.tile_pool(name="keep", bufs=1))
+        psum = ctx.enter_context(tc.psum_pool(name="psum", bufs=1))
+
+        hk_sb = keep.tile([P, H], BF16)
+        nc.sync.dma_start(out=hk_sb[:], in_=hk)
+        kw2_raw = keep.tile([P, PACK, K], BF16)
+        nc.sync.dma_start(out=kw2_raw[:], in_=kw2.rearrange("(p j) k -> p j k", j=PACK))
+        bases_rows = bases.rearrange("(p j) o i -> p j (o i)", j=PACK)
+        bases_raw = []
+        for n in range(N_TILES):
+            raw = keep.tile([P, PACK, N_TILE], BF16, name="bases_raw%d" % n)
+            nc.sync.dma_start(out=raw[:], in_=bases_rows[:, :, n * N_TILE : (n + 1) * N_TILE])
+            bases_raw.append(raw)
+
+        row_sb = keep.tile([P, O], BF16)
+        nc.scalar.dma_start(out=row_sb[:], in_=row)
+        col_sb = keep.tile([P, I], BF16)
+        nc.scalar.dma_start(out=col_sb[:], in_=col)
+        base_sb = keep.tile([P, 8], BF16)
+        nc.scalar.dma_start(out=base_sb[:], in_=base.rearrange("o (g e) -> (o g) e", e=8))
+        kb2_sb = keep.tile([P, PACK], BF16)
+        nc.scalar.dma_start(out=kb2_sb[:], in_=kb2.rearrange("(q s) -> q s", s=PACK))
+
+        ident = keep.tile([P, P], F32)
+        make_identity(nc, ident[:])
+        warm = keep.tile([P, 1], F32)
+        nc.vector.memset(warm[:], 0.0)
+        nc.scalar.activation(out=warm[:], in_=warm[:], func=TANH)
+
+        hk_words = hk_sb[:].bitcast(F32).rearrange("b (p u) -> b u p", u=2)
+        hkT_ps = psum.tile([P, 2, B], F32)
+        for u in range(2):
+            nc.tensor.transpose(hkT_ps[:, u, :], hk_words[:, u, :], ident[:])
+        hk_grouped = keep.tile([P, B * PACK], BF16, align_bytes=64)
+        nc.vector.tensor_copy(
+            out=hk_grouped[:].bitcast(F32).rearrange("p (b u) -> p b u", u=2),
+            in_=hkT_ps[:].rearrange("p u b -> p b u"),
+        )
+        hk_codes = keep.tile([P, B], U32, align_bytes=64)
+        hk_scales = keep.tile([P, B], U8, align_bytes=64)
+        nc.vector.quantize_mx(out=hk_codes[:].bitcast(FP8X4), scales=hk_scales[:], in_=hk_grouped[:])
+
+        base_words = base_sb[:].bitcast(F32)
+        base_ps = psum.tile([P, 4, P], F32)
+        for m in range(4):
+            nc.tensor.transpose(base_ps[:, m, :], base_words[:, m : m + 1].to_broadcast([P, P]), ident[:])
+        base_all = keep.tile([P, OI], BF16)
+        nc.scalar.copy(
+            out=base_all[:].bitcast(F32).rearrange("c (q m) -> c q m", m=4),
+            in_=base_ps[:].rearrange("c m q -> c q m"),
+        )
+
+        gains = keep.tile([P, O, I], F32)
+        nc.vector.tensor_tensor(
+            out=gains[:],
+            in0=row_sb[:].unsqueeze(2).to_broadcast([P, O, I]),
+            in1=col_sb[:].unsqueeze(1).to_broadcast([P, O, I]),
+            op=MULT,
+        )
+        gains_flat = gains[:].rearrange("b o i -> b (o i)")
+
+        kw2_grouped = keep.tile([P, K, PACK], BF16, align_bytes=64)
+        kw2_codes = keep.tile([P, K], U32, align_bytes=64)
+        kw2_scales = keep.tile([P, K], U8, align_bytes=64)
+        kw2_dst = kw2_grouped[:].rearrange("p (s q) j -> p s q j", s=PACK)
+        kw2_src = kw2_raw[:].rearrange("p j (q s) -> p s q j", s=PACK)
+        nc.vector.tensor_copy(out=kw2_dst[:, 0:2], in_=kw2_src[:, 0:2])
+        nc.scalar.copy(out=kw2_dst[:, 2:4], in_=kw2_src[:, 2:4])
+        nc.vector.quantize_mx(
+            out=kw2_codes[:].bitcast(FP8X4),
+            scales=kw2_scales[:],
+            in_=kw2_grouped[:].rearrange("p c j -> p (c j)"),
+        )
+
+        z_ps = psum.tile([P, PACK, B], F32)
+        for s in range(PACK):
+            nc.tensor.matmul_mx(
+                out=z_ps[:, s, :],
+                lhsT=kw2_codes[:, s * P : (s + 1) * P].bitcast(FP8X4),
+                lhsT_scale=kw2_scales[:, s * P : (s + 1) * P],
+                rhs=hk_codes[:].bitcast(FP8X4),
+                rhs_scale=hk_scales[:],
+                start=True,
+                stop=True,
+            )
+        coeffT = keep.tile([P, PACK, B], F32)
+        for s in range(PACK):
+            nc.scalar.activation(
+                out=coeffT[:, s, :], in_=z_ps[:, s, :], func=TANH, bias=kb2_sb[:, s : s + 1], scale=1.0
+            )
+
+        coeff_grouped = keep.tile([P, B, PACK], BF16, align_bytes=64)
+        nc.vector.tensor_copy(out=coeff_grouped[:], in_=coeffT[:].rearrange("q s b -> q b s"))
+        coeff_codes = keep.tile([P, B], U32, align_bytes=64)
+        coeff_scales = keep.tile([P, B], U8, align_bytes=64)
+        nc.vector.quantize_mx(
+            out=coeff_codes[:].bitcast(FP8X4),
+            scales=coeff_scales[:],
+            in_=coeff_grouped[:].rearrange("q b s -> q (b s)"),
+        )
+
+        coeff_ps = psum.tile([P, PACK, P], F32)
+        for s in range(PACK):
+            nc.tensor.transpose(coeff_ps[:, s, :], coeffT[:, s, :], ident[:])
+        coeff_sb = keep.tile([P, K], F32)
+        nc.scalar.copy(
+            out=coeff_sb[:].rearrange("b (q s) -> b q s", s=PACK),
+            in_=coeff_ps[:].rearrange("b s q -> b q s"),
+        )
+        nc.scalar.dma_start(out=coeff, in_=coeff_sb[:])
+
+        weight_flat = weight.rearrange("b o i -> b (o i)")
+        half = N_TILE // 2
+        for n in range(N_TILES):
+            cols = slice(n * N_TILE, (n + 1) * N_TILE)
+            grouped = keep.tile([P, N_TILE, PACK], BF16, align_bytes=64, name="bases_grouped%d" % n)
+            regroup(nc.vector.tensor_copy, grouped, bases_raw[n], slice(0, half))
+            regroup(nc.scalar.copy, grouped, bases_raw[n], slice(half, N_TILE))
+            codes = keep.tile([P, N_TILE], U32, align_bytes=64, name="bases_codes%d" % n)
+            scales = keep.tile([P, N_TILE], U8, align_bytes=64, name="bases_scales%d" % n)
+            nc.vector.quantize_mx(
+                out=codes[:].bitcast(FP8X4), scales=scales[:], in_=grouped[:].rearrange("p c j -> p (c j)")
+            )
+            delta_ps = psum.tile([P, N_TILE], F32, name="delta_ps%d" % n)
+            nc.tensor.matmul_mx(
+                out=delta_ps[:],
+                lhsT=coeff_codes[:].bitcast(FP8X4),
+                lhsT_scale=coeff_scales[:],
+                rhs=codes[:].bitcast(FP8X4),
+                rhs_scale=scales[:],
+                start=True,
+                stop=True,
+            )
+            summed = keep.tile([P, N_TILE], F32, name="summed%d" % n)
+            nc.vector.tensor_tensor(out=summed[:], in0=delta_ps[:], in1=base_all[:, cols], op=ADD)
+            weight_sb = keep.tile([P, N_TILE], F32, name="weight_sb%d" % n)
+            nc.vector.tensor_tensor(out=weight_sb[:], in0=summed[:], in1=gains_flat[:, cols], op=MULT)
+            nc.sync.dma_start(out=weight_flat[:, cols], in_=weight_sb[:])

@@ -22,6 +22,8 @@ RUN = 4
 
 FLOPS = 2 * B * H * K + 2 * B * K * OI
 
+V_COLS = 256
+
 
 def regroup(engine_copy, grouped, raw, cols):
     engine_copy(
@@ -37,11 +39,26 @@ def tile_structuredternaryfactorgenerator_pa_s_kernel(
     with ExitStack() as ctx:
         keep = ctx.enter_context(tc.tile_pool(name="keep", bufs=1))
         psum = ctx.enter_context(tc.psum_pool(name="psum", bufs=1))
+        ctx.enter_context(tc.manual_schedule())
+
+        def quantise(name, grouped_flat, width):
+            codes = keep.tile([P, width], U32, align_bytes=64, name=name + "_codes")
+            scales = keep.tile([P, width], U8, align_bytes=64, name=name + "_scales")
+            nc.vector.quantize_mx(out=codes[:].bitcast(FP8X4), scales=scales[:], in_=grouped_flat)
+            return codes, scales
 
         hk_sb = keep.tile([P, H], BF16)
         nc.sync.dma_start(out=hk_sb[:], in_=hk)
+        row_sb = keep.tile([P, O], BF16)
+        nc.sync.dma_start(out=row_sb[:], in_=row)
+        col_sb = keep.tile([P, I], BF16)
+        nc.sync.dma_start(out=col_sb[:], in_=col)
         kw2_raw = keep.tile([P, PACK, K], BF16)
         nc.sync.dma_start(out=kw2_raw[:], in_=kw2.rearrange("(p j) k -> p j k", j=PACK))
+        base_sb = keep.tile([P, 8], BF16)
+        nc.sync.dma_start(out=base_sb[:], in_=base.rearrange("o (g e) -> (o g) e", e=8))
+        kb2_sb = keep.tile([P, PACK], BF16)
+        nc.sync.dma_start(out=kb2_sb[:], in_=kb2.rearrange("(q s) -> q s", s=PACK))
         bases_rows = bases.rearrange("(p j) o i -> p j (o i)", j=PACK)
         bases_raw = []
         for n in range(N_TILES):
@@ -49,20 +66,26 @@ def tile_structuredternaryfactorgenerator_pa_s_kernel(
             nc.sync.dma_start(out=raw[:], in_=bases_rows[:, :, n * N_TILE : (n + 1) * N_TILE])
             bases_raw.append(raw)
 
-        row_sb = keep.tile([P, O], BF16)
-        nc.scalar.dma_start(out=row_sb[:], in_=row)
-        col_sb = keep.tile([P, I], BF16)
-        nc.scalar.dma_start(out=col_sb[:], in_=col)
-        base_sb = keep.tile([P, 8], BF16)
-        nc.scalar.dma_start(out=base_sb[:], in_=base.rearrange("o (g e) -> (o g) e", e=8))
-        kb2_sb = keep.tile([P, PACK], BF16)
-        nc.scalar.dma_start(out=kb2_sb[:], in_=kb2.rearrange("(q s) -> q s", s=PACK))
-
         ident = keep.tile([P, P], F32)
         make_identity(nc, ident[:])
         warm = keep.tile([P, 1], F32)
         nc.vector.memset(warm[:], 0.0)
         nc.scalar.activation(out=warm[:], in_=warm[:], func=TANH)
+
+        gains = keep.tile([P, O, I], F32)
+        nc.vector.tensor_tensor(
+            out=gains[:],
+            in0=row_sb[:].unsqueeze(2).to_broadcast([P, O, I]),
+            in1=col_sb[:].unsqueeze(1).to_broadcast([P, O, I]),
+            op=MULT,
+        )
+        gains_flat = gains[:].rearrange("b o i -> b (o i)")
+
+        kw2_grouped = keep.tile([P, PACK, P * PACK], BF16, align_bytes=64)
+        kw2_dst = kw2_grouped[:].rearrange("p s (q j) -> p s q j", j=PACK)
+        kw2_src = kw2_raw[:].rearrange("p j (q s) -> p s q j", s=PACK)
+        nc.vector.tensor_copy(out=kw2_dst[:, 0:2], in_=kw2_src[:, 0:2])
+        nc.scalar.copy(out=kw2_dst[:, 2:4], in_=kw2_src[:, 2:4])
 
         hk_words = hk_sb[:].bitcast(F32).rearrange("b (p u) -> b u p", u=2)
         hkT_ps = psum.tile([P, 2, B], F32)
@@ -73,9 +96,6 @@ def tile_structuredternaryfactorgenerator_pa_s_kernel(
             out=hk_grouped[:].bitcast(F32).rearrange("p (b u) -> p b u", u=2),
             in_=hkT_ps[:].rearrange("p u b -> p b u"),
         )
-        hk_codes = keep.tile([P, B], U32, align_bytes=64)
-        hk_scales = keep.tile([P, B], U8, align_bytes=64)
-        nc.vector.quantize_mx(out=hk_codes[:].bitcast(FP8X4), scales=hk_scales[:], in_=hk_grouped[:])
 
         base_words = base_sb[:].bitcast(F32)
         base_ps = psum.tile([P, 4, P], F32)
@@ -87,54 +107,42 @@ def tile_structuredternaryfactorgenerator_pa_s_kernel(
             in_=base_ps[:].rearrange("c m q -> c q m"),
         )
 
-        gains = keep.tile([P, O, I], F32)
-        nc.vector.tensor_tensor(
-            out=gains[:],
-            in0=row_sb[:].unsqueeze(2).to_broadcast([P, O, I]),
-            in1=col_sb[:].unsqueeze(1).to_broadcast([P, O, I]),
-            op=MULT,
-        )
-        gains_flat = gains[:].rearrange("b o i -> b (o i)")
-
-        kw2_grouped = keep.tile([P, K, PACK], BF16, align_bytes=64)
-        kw2_codes = keep.tile([P, K], U32, align_bytes=64)
-        kw2_scales = keep.tile([P, K], U8, align_bytes=64)
-        kw2_dst = kw2_grouped[:].rearrange("p (s q) j -> p s q j", s=PACK)
-        kw2_src = kw2_raw[:].rearrange("p j (q s) -> p s q j", s=PACK)
-        nc.vector.tensor_copy(out=kw2_dst[:, 0:2], in_=kw2_src[:, 0:2])
-        nc.scalar.copy(out=kw2_dst[:, 2:4], in_=kw2_src[:, 2:4])
-        nc.vector.quantize_mx(
-            out=kw2_codes[:].bitcast(FP8X4),
-            scales=kw2_scales[:],
-            in_=kw2_grouped[:].rearrange("p c j -> p (c j)"),
-        )
-
-        z_ps = psum.tile([P, PACK, B], F32)
-        for s in range(PACK):
-            nc.tensor.matmul_mx(
-                out=z_ps[:, s, :],
-                lhsT=kw2_codes[:, s * P : (s + 1) * P].bitcast(FP8X4),
-                lhsT_scale=kw2_scales[:, s * P : (s + 1) * P],
-                rhs=hk_codes[:].bitcast(FP8X4),
-                rhs_scale=hk_scales[:],
-                start=True,
-                stop=True,
-            )
+        kw2_mx = [quantise("kw2_0", kw2_grouped[:, 0:2, :].rearrange("p s c -> p (s c)"), 2 * P)]
+        hk_codes, hk_scales = quantise("hk", hk_grouped[:], B)
+        kw2_mx.append(quantise("kw2_1", kw2_grouped[:, 2:4, :].rearrange("p s c -> p (s c)"), 2 * P))
         coeffT = keep.tile([P, PACK, B], F32)
-        for s in range(PACK):
-            nc.scalar.activation(
-                out=coeffT[:, s, :], in_=z_ps[:, s, :], func=TANH, bias=kb2_sb[:, s : s + 1], scale=1.0
-            )
+        for pair in range(2):
+            codes, scales = kw2_mx[pair]
+            z_ps = psum.tile([P, 2, B], F32, name="z_ps%d" % pair)
+            for e in range(2):
+                nc.tensor.matmul_mx(
+                    out=z_ps[:, e, :],
+                    lhsT=codes[:, e * P : (e + 1) * P].bitcast(FP8X4),
+                    lhsT_scale=scales[:, e * P : (e + 1) * P],
+                    rhs=hk_codes[:].bitcast(FP8X4),
+                    rhs_scale=hk_scales[:],
+                    start=True,
+                    stop=True,
+                )
+            for e in range(2):
+                s = 2 * pair + e
+                nc.scalar.activation(
+                    out=coeffT[:, s, :], in_=z_ps[:, e, :], func=TANH, bias=kb2_sb[:, s : s + 1], scale=1.0
+                )
+
+        bases_grouped = []
+        for n in range(N_TILES):
+            grouped = keep.tile([P, N_TILE, PACK], BF16, align_bytes=64, name="bases_grouped%d" % n)
+            bases_grouped.append(grouped)
+            regroup(nc.scalar.copy, grouped, bases_raw[n], slice(V_COLS, N_TILE))
+        regroup(nc.vector.tensor_copy, bases_grouped[0], bases_raw[0], slice(0, V_COLS))
 
         coeff_grouped = keep.tile([P, B, PACK], BF16, align_bytes=64)
-        nc.vector.tensor_copy(out=coeff_grouped[:], in_=coeffT[:].rearrange("q s b -> q b s"))
-        coeff_codes = keep.tile([P, B], U32, align_bytes=64)
-        coeff_scales = keep.tile([P, B], U8, align_bytes=64)
-        nc.vector.quantize_mx(
-            out=coeff_codes[:].bitcast(FP8X4),
-            scales=coeff_scales[:],
-            in_=coeff_grouped[:].rearrange("q b s -> q (b s)"),
-        )
+        for pair in range(2):
+            ss = slice(2 * pair, 2 * pair + 2)
+            nc.vector.tensor_copy(out=coeff_grouped[:, :, ss], in_=coeffT[:, ss, :].rearrange("q s b -> q b s"))
+        regroup(nc.vector.tensor_copy, bases_grouped[1], bases_raw[1], slice(0, V_COLS))
+        coeff_codes, coeff_scales = quantise("coeff", coeff_grouped[:].rearrange("q b s -> q (b s)"), B)
 
         coeff_ps = psum.tile([P, PACK, P], F32)
         for s in range(PACK):
@@ -146,21 +154,13 @@ def tile_structuredternaryfactorgenerator_pa_s_kernel(
         )
         nc.scalar.dma_start(out=coeff, in_=coeff_sb[:])
 
-        weight_flat = weight.rearrange("b o i -> b (o i)")
-        half = N_TILE // 2
+        delta_ps = []
         for n in range(N_TILES):
-            cols = slice(n * N_TILE, (n + 1) * N_TILE)
-            grouped = keep.tile([P, N_TILE, PACK], BF16, align_bytes=64, name="bases_grouped%d" % n)
-            regroup(nc.vector.tensor_copy, grouped, bases_raw[n], slice(0, half))
-            regroup(nc.scalar.copy, grouped, bases_raw[n], slice(half, N_TILE))
-            codes = keep.tile([P, N_TILE], U32, align_bytes=64, name="bases_codes%d" % n)
-            scales = keep.tile([P, N_TILE], U8, align_bytes=64, name="bases_scales%d" % n)
-            nc.vector.quantize_mx(
-                out=codes[:].bitcast(FP8X4), scales=scales[:], in_=grouped[:].rearrange("p c j -> p (c j)")
-            )
-            delta_ps = psum.tile([P, N_TILE], F32, name="delta_ps%d" % n)
+            codes, scales = quantise("bases%d" % n, bases_grouped[n][:].rearrange("p c j -> p (c j)"), N_TILE)
+            acc = psum.tile([P, N_TILE], F32, name="delta_ps%d" % n)
+            delta_ps.append(acc)
             nc.tensor.matmul_mx(
-                out=delta_ps[:],
+                out=acc[:],
                 lhsT=coeff_codes[:].bitcast(FP8X4),
                 lhsT_scale=coeff_scales[:],
                 rhs=codes[:].bitcast(FP8X4),
@@ -168,8 +168,12 @@ def tile_structuredternaryfactorgenerator_pa_s_kernel(
                 start=True,
                 stop=True,
             )
+
+        weight_flat = weight.rearrange("b o i -> b (o i)")
+        for n in range(N_TILES):
+            cols = slice(n * N_TILE, (n + 1) * N_TILE)
             summed = keep.tile([P, N_TILE], F32, name="summed%d" % n)
-            nc.vector.tensor_tensor(out=summed[:], in0=delta_ps[:], in1=base_all[:, cols], op=ADD)
+            nc.vector.tensor_tensor(out=summed[:], in0=delta_ps[n][:], in1=base_all[:, cols], op=ADD)
             weight_sb = keep.tile([P, N_TILE], F32, name="weight_sb%d" % n)
             nc.vector.tensor_tensor(out=weight_sb[:], in0=summed[:], in1=gains_flat[:, cols], op=MULT)
             nc.sync.dma_start(out=weight_flat[:, cols], in_=weight_sb[:])

@@ -11,6 +11,7 @@ FP8X4 = mybir.dt.float8_e4m3fn_x4
 ADD = mybir.AluOpType.add
 MULT = mybir.AluOpType.mult
 TANH = mybir.ActivationFunctionType.Tanh
+COPY = mybir.ActivationFunctionType.Copy
 
 P = 128
 PACK = 4
@@ -22,7 +23,7 @@ RUN = 4
 
 FLOPS = 2 * B * H * K + 2 * B * K * OI
 
-V_COLS = 256
+V_COLS = 128
 
 
 def regroup(engine_copy, grouped, raw, cols):
@@ -49,10 +50,6 @@ def tile_structuredternaryfactorgenerator_pa_s_kernel(
 
         hk_sb = keep.tile([P, H], BF16)
         nc.sync.dma_start(out=hk_sb[:], in_=hk)
-        row_sb = keep.tile([P, O], BF16)
-        nc.sync.dma_start(out=row_sb[:], in_=row)
-        col_sb = keep.tile([P, I], BF16)
-        nc.sync.dma_start(out=col_sb[:], in_=col)
         kw2_raw = keep.tile([P, PACK, K], BF16)
         nc.sync.dma_start(out=kw2_raw[:], in_=kw2.rearrange("(p j) k -> p j k", j=PACK))
         base_sb = keep.tile([P, 8], BF16)
@@ -65,6 +62,10 @@ def tile_structuredternaryfactorgenerator_pa_s_kernel(
             raw = keep.tile([P, PACK, N_TILE], BF16, name="bases_raw%d" % n)
             nc.sync.dma_start(out=raw[:], in_=bases_rows[:, :, n * N_TILE : (n + 1) * N_TILE])
             bases_raw.append(raw)
+        row_sb = keep.tile([P, O], BF16)
+        nc.sync.dma_start(out=row_sb[:], in_=row)
+        col_sb = keep.tile([P, I], BF16)
+        nc.sync.dma_start(out=col_sb[:], in_=col)
 
         ident = keep.tile([P, P], F32)
         make_identity(nc, ident[:])
@@ -72,20 +73,10 @@ def tile_structuredternaryfactorgenerator_pa_s_kernel(
         nc.vector.memset(warm[:], 0.0)
         nc.scalar.activation(out=warm[:], in_=warm[:], func=TANH)
 
+        row_f32 = keep.tile([P, O], F32)
         gains = keep.tile([P, O, I], F32)
-        nc.vector.tensor_tensor(
-            out=gains[:],
-            in0=row_sb[:].unsqueeze(2).to_broadcast([P, O, I]),
-            in1=col_sb[:].unsqueeze(1).to_broadcast([P, O, I]),
-            op=MULT,
-        )
         gains_flat = gains[:].rearrange("b o i -> b (o i)")
 
-        kw2_grouped = keep.tile([P, PACK, P * PACK], BF16, align_bytes=64)
-        kw2_dst = kw2_grouped[:].rearrange("p s (q j) -> p s q j", j=PACK)
-        kw2_src = kw2_raw[:].rearrange("p j (q s) -> p s q j", s=PACK)
-        nc.vector.tensor_copy(out=kw2_dst[:, 0:2], in_=kw2_src[:, 0:2])
-        nc.scalar.copy(out=kw2_dst[:, 2:4], in_=kw2_src[:, 2:4])
 
         hk_words = hk_sb[:].bitcast(F32).rearrange("b (p u) -> b u p", u=2)
         hkT_ps = psum.tile([P, 2, B], F32)
@@ -96,6 +87,13 @@ def tile_structuredternaryfactorgenerator_pa_s_kernel(
             out=hk_grouped[:].bitcast(F32).rearrange("p (b u) -> p b u", u=2),
             in_=hkT_ps[:].rearrange("p u b -> p b u"),
         )
+
+        kw2_grouped = keep.tile([P, PACK, P * PACK], BF16, align_bytes=64)
+        kw2_dst = kw2_grouped[:].rearrange("p s (q j) -> p s q j", j=PACK)
+        kw2_src = kw2_raw[:].rearrange("p j (q s) -> p s q j", s=PACK)
+        nc.vector.tensor_copy(out=kw2_dst[:, 0:2], in_=kw2_src[:, 0:2])
+        nc.scalar.copy(out=kw2_dst[:, 2:4], in_=kw2_src[:, 2:4])
+        hk_codes, hk_scales = quantise("hk", hk_grouped[:], B)
 
         base_words = base_sb[:].bitcast(F32)
         base_ps = psum.tile([P, 4, P], F32)
@@ -108,7 +106,6 @@ def tile_structuredternaryfactorgenerator_pa_s_kernel(
         )
 
         kw2_mx = [quantise("kw2_0", kw2_grouped[:, 0:2, :].rearrange("p s c -> p (s c)"), 2 * P)]
-        hk_codes, hk_scales = quantise("hk", hk_grouped[:], B)
         kw2_mx.append(quantise("kw2_1", kw2_grouped[:, 2:4, :].rearrange("p s c -> p (s c)"), 2 * P))
         coeffT = keep.tile([P, PACK, B], F32)
         for pair in range(2):
@@ -134,15 +131,20 @@ def tile_structuredternaryfactorgenerator_pa_s_kernel(
         for n in range(N_TILES):
             grouped = keep.tile([P, N_TILE, PACK], BF16, align_bytes=64, name="bases_grouped%d" % n)
             bases_grouped.append(grouped)
-            regroup(nc.scalar.copy, grouped, bases_raw[n], slice(V_COLS, N_TILE))
-        regroup(nc.vector.tensor_copy, bases_grouped[0], bases_raw[0], slice(0, V_COLS))
+        regroup(nc.vector.tensor_copy, bases_grouped[0], bases_raw[0], slice(0, N_TILE))
+        regroup(nc.scalar.copy, bases_grouped[1], bases_raw[1], slice(V_COLS, N_TILE))
+        nc.scalar.copy(out=row_f32[:], in_=row_sb[:])
+        for o in range(O):
+            nc.scalar.activation(out=gains[:, o, :], in_=col_sb[:], func=COPY, scale=row_f32[:, o : o + 1])
 
         coeff_grouped = keep.tile([P, B, PACK], BF16, align_bytes=64)
         for pair in range(2):
             ss = slice(2 * pair, 2 * pair + 2)
             nc.vector.tensor_copy(out=coeff_grouped[:, :, ss], in_=coeffT[:, ss, :].rearrange("q s b -> q b s"))
-        regroup(nc.vector.tensor_copy, bases_grouped[1], bases_raw[1], slice(0, V_COLS))
+        bases_mx = [quantise("bases0", bases_grouped[0][:].rearrange("p c j -> p (c j)"), N_TILE)]
         coeff_codes, coeff_scales = quantise("coeff", coeff_grouped[:].rearrange("q b s -> q (b s)"), B)
+        regroup(nc.vector.tensor_copy, bases_grouped[1], bases_raw[1], slice(0, V_COLS))
+        bases_mx.append(quantise("bases1", bases_grouped[1][:].rearrange("p c j -> p (c j)"), N_TILE))
 
         coeff_ps = psum.tile([P, PACK, P], F32)
         for s in range(PACK):
@@ -156,7 +158,7 @@ def tile_structuredternaryfactorgenerator_pa_s_kernel(
 
         delta_ps = []
         for n in range(N_TILES):
-            codes, scales = quantise("bases%d" % n, bases_grouped[n][:].rearrange("p c j -> p (c j)"), N_TILE)
+            codes, scales = bases_mx[n]
             acc = psum.tile([P, N_TILE], F32, name="delta_ps%d" % n)
             delta_ps.append(acc)
             nc.tensor.matmul_mx(

@@ -11,7 +11,6 @@ FP8X4 = mybir.dt.float8_e4m3fn_x4
 ADD = mybir.AluOpType.add
 MULT = mybir.AluOpType.mult
 TANH = mybir.ActivationFunctionType.Tanh
-COPY = mybir.ActivationFunctionType.Copy
 
 P = 128
 PACK = 4
@@ -23,6 +22,7 @@ RUN = 4
 
 FLOPS = 2 * B * H * K + 2 * B * K * OI
 
+STORE_COLS = 256
 V_COLS = 128
 
 
@@ -48,6 +48,10 @@ def tile_structuredternaryfactorgenerator_pa_s_kernel(
             nc.vector.quantize_mx(out=codes[:].bitcast(FP8X4), scales=scales[:], in_=grouped_flat)
             return codes, scales
 
+        row_sb = keep.tile([P, O], BF16)
+        nc.sync.dma_start(out=row_sb[:], in_=row)
+        col_sb = keep.tile([P, I], BF16)
+        nc.sync.dma_start(out=col_sb[:], in_=col)
         hk_sb = keep.tile([P, H], BF16)
         nc.sync.dma_start(out=hk_sb[:], in_=hk)
         kw2_raw = keep.tile([P, PACK, K], BF16)
@@ -62,10 +66,6 @@ def tile_structuredternaryfactorgenerator_pa_s_kernel(
             raw = keep.tile([P, PACK, N_TILE], BF16, name="bases_raw%d" % n)
             nc.sync.dma_start(out=raw[:], in_=bases_rows[:, :, n * N_TILE : (n + 1) * N_TILE])
             bases_raw.append(raw)
-        row_sb = keep.tile([P, O], BF16)
-        nc.sync.dma_start(out=row_sb[:], in_=row)
-        col_sb = keep.tile([P, I], BF16)
-        nc.sync.dma_start(out=col_sb[:], in_=col)
 
         ident = keep.tile([P, P], F32)
         make_identity(nc, ident[:])
@@ -73,8 +73,13 @@ def tile_structuredternaryfactorgenerator_pa_s_kernel(
         nc.vector.memset(warm[:], 0.0)
         nc.scalar.activation(out=warm[:], in_=warm[:], func=TANH)
 
-        row_f32 = keep.tile([P, O], F32)
         gains = keep.tile([P, O, I], F32)
+        nc.vector.tensor_tensor(
+            out=gains[:],
+            in0=row_sb[:].unsqueeze(2).to_broadcast([P, O, I]),
+            in1=col_sb[:].unsqueeze(1).to_broadcast([P, O, I]),
+            op=MULT,
+        )
         gains_flat = gains[:].rearrange("b o i -> b (o i)")
 
 
@@ -133,9 +138,6 @@ def tile_structuredternaryfactorgenerator_pa_s_kernel(
             bases_grouped.append(grouped)
         regroup(nc.vector.tensor_copy, bases_grouped[0], bases_raw[0], slice(0, N_TILE))
         regroup(nc.scalar.copy, bases_grouped[1], bases_raw[1], slice(V_COLS, N_TILE))
-        nc.scalar.copy(out=row_f32[:], in_=row_sb[:])
-        for o in range(O):
-            nc.scalar.activation(out=gains[:, o, :], in_=col_sb[:], func=COPY, scale=row_f32[:, o : o + 1])
 
         coeff_grouped = keep.tile([P, B, PACK], BF16, align_bytes=64)
         for pair in range(2):
@@ -173,9 +175,14 @@ def tile_structuredternaryfactorgenerator_pa_s_kernel(
 
         weight_flat = weight.rearrange("b o i -> b (o i)")
         for n in range(N_TILES):
-            cols = slice(n * N_TILE, (n + 1) * N_TILE)
             summed = keep.tile([P, N_TILE], F32, name="summed%d" % n)
-            nc.vector.tensor_tensor(out=summed[:], in0=delta_ps[n][:], in1=base_all[:, cols], op=ADD)
-            weight_sb = keep.tile([P, N_TILE], F32, name="weight_sb%d" % n)
-            nc.vector.tensor_tensor(out=weight_sb[:], in0=summed[:], in1=gains_flat[:, cols], op=MULT)
-            nc.sync.dma_start(out=weight_flat[:, cols], in_=weight_sb[:])
+            nc.vector.tensor_tensor(
+                out=summed[:], in0=delta_ps[n][:], in1=base_all[:, n * N_TILE : (n + 1) * N_TILE], op=ADD
+            )
+            for first in range(0, N_TILE, STORE_COLS):
+                cols = slice(n * N_TILE + first, n * N_TILE + first + STORE_COLS)
+                weight_sb = keep.tile([P, STORE_COLS], F32, name="weight_sb%d_%d" % (n, first))
+                nc.vector.tensor_tensor(
+                    out=weight_sb[:], in0=summed[:, first : first + STORE_COLS], in1=gains_flat[:, cols], op=MULT
+                )
+                nc.sync.dma_start(out=weight_flat[:, cols], in_=weight_sb[:])

@@ -22,8 +22,10 @@ RUN = 4
 
 FLOPS = 2 * B * H * K + 2 * B * K * OI
 
-STORE_COLS = 256
-V_COLS = 128
+PIECE = 256
+PIECES = OI // PIECE
+S_COLS = 192
+V_COLS = 192
 
 
 def regroup(engine_copy, grouped, raw, cols):
@@ -104,11 +106,12 @@ def tile_structuredternaryfactorgenerator_pa_s_kernel(
         base_ps = psum.tile([P, 4, P], F32)
         for m in range(4):
             nc.tensor.transpose(base_ps[:, m, :], base_words[:, m : m + 1].to_broadcast([P, P]), ident[:])
-        base_all = keep.tile([P, OI], BF16)
-        nc.scalar.copy(
-            out=base_all[:].bitcast(F32).rearrange("c (q m) -> c q m", m=4),
-            in_=base_ps[:].rearrange("c m q -> c q m"),
-        )
+
+        bases_grouped = []
+        for n in range(N_TILES):
+            grouped = keep.tile([P, N_TILE, PACK], BF16, align_bytes=64, name="bases_grouped%d" % n)
+            bases_grouped.append(grouped)
+        regroup(nc.scalar.copy, bases_grouped[0], bases_raw[0], slice(0, S_COLS))
 
         kw2_mx = [quantise("kw2_0", kw2_grouped[:, 0:2, :].rearrange("p s c -> p (s c)"), 2 * P)]
         kw2_mx.append(quantise("kw2_1", kw2_grouped[:, 2:4, :].rearrange("p s c -> p (s c)"), 2 * P))
@@ -132,12 +135,14 @@ def tile_structuredternaryfactorgenerator_pa_s_kernel(
                     out=coeffT[:, s, :], in_=z_ps[:, e, :], func=TANH, bias=kb2_sb[:, s : s + 1], scale=1.0
                 )
 
-        bases_grouped = []
-        for n in range(N_TILES):
-            grouped = keep.tile([P, N_TILE, PACK], BF16, align_bytes=64, name="bases_grouped%d" % n)
-            bases_grouped.append(grouped)
-        regroup(nc.vector.tensor_copy, bases_grouped[0], bases_raw[0], slice(0, N_TILE))
+        regroup(nc.vector.tensor_copy, bases_grouped[0], bases_raw[0], slice(S_COLS, N_TILE))
+        regroup(nc.vector.tensor_copy, bases_grouped[1], bases_raw[1], slice(0, V_COLS))
         regroup(nc.scalar.copy, bases_grouped[1], bases_raw[1], slice(V_COLS, N_TILE))
+        base_all = keep.tile([P, OI], BF16)
+        nc.scalar.copy(
+            out=base_all[:].bitcast(F32).rearrange("c (q m) -> c q m", m=4),
+            in_=base_ps[:].rearrange("c m q -> c q m"),
+        )
 
         coeff_grouped = keep.tile([P, B, PACK], BF16, align_bytes=64)
         for pair in range(2):
@@ -145,7 +150,6 @@ def tile_structuredternaryfactorgenerator_pa_s_kernel(
             nc.vector.tensor_copy(out=coeff_grouped[:, :, ss], in_=coeffT[:, ss, :].rearrange("q s b -> q b s"))
         bases_mx = [quantise("bases0", bases_grouped[0][:].rearrange("p c j -> p (c j)"), N_TILE)]
         coeff_codes, coeff_scales = quantise("coeff", coeff_grouped[:].rearrange("q b s -> q (b s)"), B)
-        regroup(nc.vector.tensor_copy, bases_grouped[1], bases_raw[1], slice(0, V_COLS))
         bases_mx.append(quantise("bases1", bases_grouped[1][:].rearrange("p c j -> p (c j)"), N_TILE))
 
         coeff_ps = psum.tile([P, PACK, P], F32)
@@ -158,31 +162,36 @@ def tile_structuredternaryfactorgenerator_pa_s_kernel(
         )
         nc.scalar.dma_start(out=coeff, in_=coeff_sb[:])
 
+        weight_flat = weight.rearrange("b o i -> b (o i)")
+        summed = keep.tile([P, OI], F32)
         delta_ps = []
-        for n in range(N_TILES):
-            codes, scales = bases_mx[n]
-            acc = psum.tile([P, N_TILE], F32, name="delta_ps%d" % n)
+        for n in range(PIECES):
+            codes, scales = bases_mx[n * PIECE // N_TILE]
+            cols = slice(n * PIECE % N_TILE, n * PIECE % N_TILE + PIECE)
+            acc = psum.tile([P, PIECE], F32, name="z_ps%d" % n if n < 2 else "delta_ps%d" % n)
             delta_ps.append(acc)
             nc.tensor.matmul_mx(
                 out=acc[:],
                 lhsT=coeff_codes[:].bitcast(FP8X4),
                 lhsT_scale=coeff_scales[:],
-                rhs=codes[:].bitcast(FP8X4),
-                rhs_scale=scales[:],
+                rhs=codes[:, cols].bitcast(FP8X4),
+                rhs_scale=scales[:, cols],
                 start=True,
                 stop=True,
             )
 
-        weight_flat = weight.rearrange("b o i -> b (o i)")
-        for n in range(N_TILES):
-            summed = keep.tile([P, N_TILE], F32, name="summed%d" % n)
-            nc.vector.tensor_tensor(
-                out=summed[:], in0=delta_ps[n][:], in1=base_all[:, n * N_TILE : (n + 1) * N_TILE], op=ADD
-            )
-            for first in range(0, N_TILE, STORE_COLS):
-                cols = slice(n * N_TILE + first, n * N_TILE + first + STORE_COLS)
-                weight_sb = keep.tile([P, STORE_COLS], F32, name="weight_sb%d_%d" % (n, first))
-                nc.vector.tensor_tensor(
-                    out=weight_sb[:], in0=summed[:, first : first + STORE_COLS], in1=gains_flat[:, cols], op=MULT
-                )
-                nc.sync.dma_start(out=weight_flat[:, cols], in_=weight_sb[:])
+        def add_base(n):
+            cols = slice(n * PIECE, (n + 1) * PIECE)
+            nc.vector.tensor_tensor(out=summed[:, cols], in0=delta_ps[n][:], in1=base_all[:, cols], op=ADD)
+
+        def scale_and_store(n):
+            cols = slice(n * PIECE, (n + 1) * PIECE)
+            weight_sb = keep.tile([P, PIECE], F32, name="weight_sb%d" % n)
+            nc.vector.tensor_tensor(out=weight_sb[:], in0=summed[:, cols], in1=gains_flat[:, cols], op=MULT)
+            nc.sync.dma_start(out=weight_flat[:, cols], in_=weight_sb[:])
+
+        add_base(0)
+        for n in range(1, PIECES):
+            add_base(n)
+            scale_and_store(n - 1)
+        scale_and_store(PIECES - 1)

@@ -58,16 +58,17 @@ def tile_structuredternaryfactorgenerator_pa_s_kernel(
         nc.sync.dma_start(out=hk_sb[:], in_=hk)
         kw2_raw = keep.tile([P, PACK, K], BF16)
         nc.sync.dma_start(out=kw2_raw[:], in_=kw2.rearrange("(p j) k -> p j k", j=PACK))
-        base_sb = keep.tile([P, 8], BF16)
-        nc.sync.dma_start(out=base_sb[:], in_=base.rearrange("o (g e) -> (o g) e", e=8))
-        kb2_sb = keep.tile([P, PACK], BF16)
-        nc.sync.dma_start(out=kb2_sb[:], in_=kb2.rearrange("(q s) -> q s", s=PACK))
         bases_rows = bases.rearrange("(p j) o i -> p j (o i)", j=PACK)
         bases_raw = []
         for n in range(N_TILES):
             raw = keep.tile([P, PACK, N_TILE], BF16, name="bases_raw%d" % n)
             nc.sync.dma_start(out=raw[:], in_=bases_rows[:, :, n * N_TILE : (n + 1) * N_TILE])
             bases_raw.append(raw)
+            if n == 0:
+                kb2_sb = keep.tile([P, PACK], BF16)
+                nc.sync.dma_start(out=kb2_sb[:], in_=kb2.rearrange("(q s) -> q s", s=PACK))
+        base_sb = keep.tile([P, 8], BF16)
+        nc.sync.dma_start(out=base_sb[:], in_=base.rearrange("o (g e) -> (o g) e", e=8))
 
         ident = keep.tile([P, P], F32)
         make_identity(nc, ident[:])
@@ -102,11 +103,6 @@ def tile_structuredternaryfactorgenerator_pa_s_kernel(
         nc.scalar.copy(out=kw2_dst[:, 2:4], in_=kw2_src[:, 2:4])
         hk_codes, hk_scales = quantise("hk", hk_grouped[:], B)
 
-        base_words = base_sb[:].bitcast(F32)
-        base_ps = psum.tile([P, 4, P], F32)
-        for m in range(4):
-            nc.tensor.transpose(base_ps[:, m, :], base_words[:, m : m + 1].to_broadcast([P, P]), ident[:])
-
         bases_grouped = []
         for n in range(N_TILES):
             grouped = keep.tile([P, N_TILE, PACK], BF16, align_bytes=64, name="bases_grouped%d" % n)
@@ -138,6 +134,11 @@ def tile_structuredternaryfactorgenerator_pa_s_kernel(
         regroup(nc.vector.tensor_copy, bases_grouped[0], bases_raw[0], slice(S_COLS, N_TILE))
         regroup(nc.vector.tensor_copy, bases_grouped[1], bases_raw[1], slice(0, V_COLS))
         regroup(nc.scalar.copy, bases_grouped[1], bases_raw[1], slice(V_COLS, N_TILE))
+
+        base_words = base_sb[:].bitcast(F32)
+        base_ps = psum.tile([P, 4, P], F32)
+        for m in range(4):
+            nc.tensor.transpose(base_ps[:, m, :], base_words[:, m : m + 1].to_broadcast([P, P]), ident[:])
         base_all = keep.tile([P, OI], BF16)
         nc.scalar.copy(
             out=base_all[:].bitcast(F32).rearrange("c (q m) -> c q m", m=4),

@@ -22,6 +22,7 @@ RUN = 4
 
 FLOPS = 2 * B * H * K + 2 * B * K * OI
 
+V_Q = 64
 PIECE = 256
 PIECES = OI // PIECE
 S_COLS = 192
@@ -100,7 +101,9 @@ def tile_structuredternaryfactorgenerator_pa_s_kernel(
         kw2_dst = kw2_grouped[:].rearrange("p s (q j) -> p s q j", j=PACK)
         kw2_src = kw2_raw[:].rearrange("p j (q s) -> p s q j", s=PACK)
         nc.vector.tensor_copy(out=kw2_dst[:, 0:2], in_=kw2_src[:, 0:2])
-        nc.scalar.copy(out=kw2_dst[:, 2:4], in_=kw2_src[:, 2:4])
+        nc.scalar.copy(out=kw2_dst[:, 3], in_=kw2_src[:, 3])
+        nc.scalar.copy(out=kw2_dst[:, 2, V_Q:], in_=kw2_src[:, 2, V_Q:])
+        nc.vector.tensor_copy(out=kw2_dst[:, 2, 0:V_Q], in_=kw2_src[:, 2, 0:V_Q])
         hk_codes, hk_scales = quantise("hk", hk_grouped[:], B)
 
         bases_grouped = []

@@ -98,12 +98,12 @@ def tile_structuredternaryfactorgenerator_pa_s_kernel(
         )
 
         kw2_grouped = keep.tile([P, PACK, P * PACK], BF16, align_bytes=64)
-        kw2_dst = kw2_grouped[:].rearrange("p s (q j) -> p s q j", j=PACK)
-        kw2_src = kw2_raw[:].rearrange("p j (q s) -> p s q j", s=PACK)
+        kw2_dst = kw2_grouped[:].rearrange("p s (c i j) -> p s c j i", i=RUN, j=PACK)
+        kw2_src = kw2_raw[:].rearrange("p j (c i s) -> p s c j i", i=RUN, s=PACK)
         nc.vector.tensor_copy(out=kw2_dst[:, 0:2], in_=kw2_src[:, 0:2])
         nc.scalar.copy(out=kw2_dst[:, 3], in_=kw2_src[:, 3])
-        nc.scalar.copy(out=kw2_dst[:, 2, V_Q:], in_=kw2_src[:, 2, V_Q:])
-        nc.vector.tensor_copy(out=kw2_dst[:, 2, 0:V_Q], in_=kw2_src[:, 2, 0:V_Q])
+        nc.scalar.copy(out=kw2_dst[:, 2, V_Q // RUN :], in_=kw2_src[:, 2, V_Q // RUN :])
+        nc.vector.tensor_copy(out=kw2_dst[:, 2, 0 : V_Q // RUN], in_=kw2_src[:, 2, 0 : V_Q // RUN])
         hk_codes, hk_scales = quantise("hk", hk_grouped[:], B)
 
         bases_grouped = []

@@ -18,6 +18,7 @@ B, H, K, O, I = 128, 512, 512, 32, 32
 OI = O * I
 N_TILE = 512
 N_TILES = OI // N_TILE
+PSUM_RUN = 2
 RUN = 4
 
 FLOPS = 2 * B * H * K + 2 * B * K * OI
@@ -25,8 +26,8 @@ FLOPS = 2 * B * H * K + 2 * B * K * OI
 V_Q = 64
 PIECE = 256
 PIECES = OI // PIECE
-S_COLS = 192
-V_COLS = 192
+S_COLS = 128
+V_COLS = 256
 
 
 def regroup(engine_copy, grouped, raw, cols):
@@ -50,6 +51,11 @@ def tile_structuredternaryfactorgenerator_pa_s_kernel(
             scales = keep.tile([P, width], U8, align_bytes=64, name=name + "_scales")
             nc.vector.quantize_mx(out=codes[:].bitcast(FP8X4), scales=scales[:], in_=grouped_flat)
             return codes, scales
+
+        def quantise_piece(n):
+            first = n * PIECE % N_TILE
+            grouped = bases_grouped[n * PIECE // N_TILE][:, first : first + PIECE, :]
+            return quantise("bases_piece%d" % n, grouped.rearrange("p c j -> p (c j)"), PIECE)
 
         row_sb = keep.tile([P, O], BF16)
         nc.sync.dma_start(out=row_sb[:], in_=row)
@@ -144,25 +150,24 @@ def tile_structuredternaryfactorgenerator_pa_s_kernel(
             nc.tensor.transpose(base_ps[:, m, :], base_words[:, m : m + 1].to_broadcast([P, P]), ident[:])
         base_all = keep.tile([P, OI], BF16)
         nc.scalar.copy(
-            out=base_all[:].bitcast(F32).rearrange("c (q m) -> c q m", m=4),
-            in_=base_ps[:].rearrange("c m q -> c q m"),
+            out=base_all[:].bitcast(F32).rearrange("c (a i m) -> c a m i", i=PSUM_RUN, m=4),
+            in_=base_ps[:].rearrange("c m (a i) -> c a m i", i=PSUM_RUN),
         )
 
         coeff_grouped = keep.tile([P, B, PACK], BF16, align_bytes=64)
-        for pair in range(2):
-            ss = slice(2 * pair, 2 * pair + 2)
-            nc.vector.tensor_copy(out=coeff_grouped[:, :, ss], in_=coeffT[:, ss, :].rearrange("q s b -> q b s"))
-        bases_mx = [quantise("bases0", bases_grouped[0][:].rearrange("p c j -> p (c j)"), N_TILE)]
+        regroup(nc.vector.tensor_copy, coeff_grouped, coeffT, slice(0, B))
+        bases_mx = [quantise_piece(0)]
         coeff_codes, coeff_scales = quantise("coeff", coeff_grouped[:].rearrange("q b s -> q (b s)"), B)
-        bases_mx.append(quantise("bases1", bases_grouped[1][:].rearrange("p c j -> p (c j)"), N_TILE))
+        for n in range(1, PIECES):
+            bases_mx.append(quantise_piece(n))
 
         coeff_ps = psum.tile([P, PACK, P], F32)
         for s in range(PACK):
             nc.tensor.transpose(coeff_ps[:, s, :], coeffT[:, s, :], ident[:])
         coeff_sb = keep.tile([P, K], F32)
         nc.scalar.copy(
-            out=coeff_sb[:].rearrange("b (q s) -> b q s", s=PACK),
-            in_=coeff_ps[:].rearrange("b s q -> b q s"),
+            out=coeff_sb[:].rearrange("b (a i s) -> b a s i", i=PSUM_RUN, s=PACK),
+            in_=coeff_ps[:].rearrange("b s (a i) -> b a s i", i=PSUM_RUN),
         )
         nc.scalar.dma_start(out=coeff, in_=coeff_sb[:])
 
@@ -170,16 +175,15 @@ def tile_structuredternaryfactorgenerator_pa_s_kernel(
         summed = keep.tile([P, OI], F32)
         delta_ps = []
         for n in range(PIECES):
-            codes, scales = bases_mx[n * PIECE // N_TILE]
-            cols = slice(n * PIECE % N_TILE, n * PIECE % N_TILE + PIECE)
+            codes, scales = bases_mx[n]
             acc = psum.tile([P, PIECE], F32, name="z_ps%d" % n if n < 2 else "delta_ps%d" % n)
             delta_ps.append(acc)
             nc.tensor.matmul_mx(
                 out=acc[:],
                 lhsT=coeff_codes[:].bitcast(FP8X4),
                 lhsT_scale=coeff_scales[:],
-                rhs=codes[:, cols].bitcast(FP8X4),
-                rhs_scale=scales[:, cols],
+                rhs=codes[:].bitcast(FP8X4),
+                rhs_scale=scales[:],
                 start=True,
                 stop=True,
             )

@@ -99,8 +99,8 @@ def tile_structuredternaryfactorgenerator_pa_s_kernel(
             nc.tensor.transpose(hkT_ps[:, u, :], hk_words[:, u, :], ident[:])
         hk_grouped = keep.tile([P, B * PACK], BF16, align_bytes=64)
         nc.vector.tensor_copy(
-            out=hk_grouped[:].bitcast(F32).rearrange("p (b u) -> p b u", u=2),
-            in_=hkT_ps[:].rearrange("p u b -> p b u"),
+            out=hk_grouped[:].bitcast(F32).rearrange("p (a i u) -> p a u i", i=PSUM_RUN, u=2),
+            in_=hkT_ps[:].rearrange("p u (a i) -> p a u i", i=PSUM_RUN),
         )
 
         kw2_grouped = keep.tile([P, PACK, P * PACK], BF16, align_bytes=64)
@@ -123,10 +123,11 @@ def tile_structuredternaryfactorgenerator_pa_s_kernel(
         coeffT = keep.tile([P, PACK, B], F32)
         for pair in range(2):
             codes, scales = kw2_mx[pair]
-            z_ps = psum.tile([P, 2, B], F32, name="z_ps%d" % pair)
+            z_ps = []
             for e in range(2):
+                z_ps.append(psum.tile([P, B], F32, name="bank%d" % (2 * pair + e)))
                 nc.tensor.matmul_mx(
-                    out=z_ps[:, e, :],
+                    out=z_ps[e][:],
                     lhsT=codes[:, e * P : (e + 1) * P].bitcast(FP8X4),
                     lhsT_scale=scales[:, e * P : (e + 1) * P],
                     rhs=hk_codes[:].bitcast(FP8X4),
@@ -137,7 +138,7 @@ def tile_structuredternaryfactorgenerator_pa_s_kernel(
             for e in range(2):
                 s = 2 * pair + e
                 nc.scalar.activation(
-                    out=coeffT[:, s, :], in_=z_ps[:, e, :], func=TANH, bias=kb2_sb[:, s : s + 1], scale=1.0
+                    out=coeffT[:, s, :], in_=z_ps[e][:], func=TANH, bias=kb2_sb[:, s : s + 1], scale=1.0
                 )
 
         regroup(nc.vector.tensor_copy, bases_grouped[0], bases_raw[0], slice(S_COLS, N_TILE))
@@ -176,7 +177,7 @@ def tile_structuredternaryfactorgenerator_pa_s_kernel(
         delta_ps = []
         for n in range(PIECES):
             codes, scales = bases_mx[n]
-            acc = psum.tile([P, PIECE], F32, name="z_ps%d" % n if n < 2 else "delta_ps%d" % n)
+            acc = psum.tile([P, PIECE], F32, name="bank%d" % n)
             delta_ps.append(acc)
             nc.tensor.matmul_mx(
                 out=acc[:],

@@ -27,7 +27,7 @@ V_Q = 64
 PIECE = 256
 PIECES = OI // PIECE
 S_COLS = 128
-V_COLS = 256
+V_COLS = 192
 
 
 def regroup(engine_copy, grouped, raw, cols):
@@ -65,6 +65,8 @@ def tile_structuredternaryfactorgenerator_pa_s_kernel(
         nc.sync.dma_start(out=hk_sb[:], in_=hk)
         kw2_raw = keep.tile([P, PACK, K], BF16)
         nc.sync.dma_start(out=kw2_raw[:], in_=kw2.rearrange("(p j) k -> p j k", j=PACK))
+        base_sb = keep.tile([P, 8], BF16)
+        nc.sync.dma_start(out=base_sb[:], in_=base.rearrange("o (g e) -> (o g) e", e=8))
         bases_rows = bases.rearrange("(p j) o i -> p j (o i)", j=PACK)
         bases_raw = []
         for n in range(N_TILES):
@@ -74,8 +76,6 @@ def tile_structuredternaryfactorgenerator_pa_s_kernel(
             if n == 0:
                 kb2_sb = keep.tile([P, PACK], BF16)
                 nc.sync.dma_start(out=kb2_sb[:], in_=kb2.rearrange("(q s) -> q s", s=PACK))
-        base_sb = keep.tile([P, 8], BF16)
-        nc.sync.dma_start(out=base_sb[:], in_=base.rearrange("o (g e) -> (o g) e", e=8))
 
         ident = keep.tile([P, P], F32)
         make_identity(nc, ident[:])
@@ -112,6 +112,11 @@ def tile_structuredternaryfactorgenerator_pa_s_kernel(
         nc.vector.tensor_copy(out=kw2_dst[:, 2, 0 : V_Q // RUN], in_=kw2_src[:, 2, 0 : V_Q // RUN])
         hk_codes, hk_scales = quantise("hk", hk_grouped[:], B)
 
+        base_words = base_sb[:].bitcast(F32)
+        base_ps = psum.tile([P, 4, P], F32)
+        for m in range(4):
+            nc.tensor.transpose(base_ps[:, m, :], base_words[:, m : m + 1].to_broadcast([P, P]), ident[:])
+
         bases_grouped = []
         for n in range(N_TILES):
             grouped = keep.tile([P, N_TILE, PACK], BF16, align_bytes=64, name="bases_grouped%d" % n)
@@ -141,23 +146,22 @@ def tile_structuredternaryfactorgenerator_pa_s_kernel(
                     out=coeffT[:, s, :], in_=z_ps[e][:], func=TANH, bias=kb2_sb[:, s : s + 1], scale=1.0
                 )
 
-        regroup(nc.vector.tensor_copy, bases_grouped[0], bases_raw[0], slice(S_COLS, N_TILE))
-        regroup(nc.vector.tensor_copy, bases_grouped[1], bases_raw[1], slice(0, V_COLS))
-        regroup(nc.scalar.copy, bases_grouped[1], bases_raw[1], slice(V_COLS, N_TILE))
+        regroup(nc.vector.tensor_copy, bases_grouped[0], bases_raw[0], slice(S_COLS, PIECE))
+        regroup(nc.vector.tensor_copy, bases_grouped[0], bases_raw[0], slice(PIECE, N_TILE))
+        regroup(nc.scalar.copy, bases_grouped[1], bases_raw[1], slice(V_COLS, PIECE))
+        regroup(nc.scalar.copy, bases_grouped[1], bases_raw[1], slice(PIECE, N_TILE))
 
-        base_words = base_sb[:].bitcast(F32)
-        base_ps = psum.tile([P, 4, P], F32)
-        for m in range(4):
-            nc.tensor.transpose(base_ps[:, m, :], base_words[:, m : m + 1].to_broadcast([P, P]), ident[:])
         base_all = keep.tile([P, OI], BF16)
-        nc.scalar.copy(
-            out=base_all[:].bitcast(F32).rearrange("c (a i m) -> c a m i", i=PSUM_RUN, m=4),
-            in_=base_ps[:].rearrange("c m (a i) -> c a m i", i=PSUM_RUN),
-        )
+        base_dst = base_all[:].bitcast(F32).rearrange("c (a i m) -> c a m i", i=PSUM_RUN, m=4)
+        base_src = base_ps[:].rearrange("c m (a i) -> c a m i", i=PSUM_RUN)
+        half = P // PSUM_RUN // 2
+        for rows in (slice(0, half), slice(half, 2 * half)):
+            nc.scalar.copy(out=base_dst[:, rows], in_=base_src[:, rows])
 
         coeff_grouped = keep.tile([P, B, PACK], BF16, align_bytes=64)
-        regroup(nc.vector.tensor_copy, coeff_grouped, coeffT, slice(0, B))
         bases_mx = [quantise_piece(0)]
+        regroup(nc.vector.tensor_copy, coeff_grouped, coeffT, slice(0, B))
+        regroup(nc.vector.tensor_copy, bases_grouped[1], bases_raw[1], slice(0, V_COLS))
         coeff_codes, coeff_scales = quantise("coeff", coeff_grouped[:].rearrange("q b s -> q (b s)"), B)
         for n in range(1, PIECES):
             bases_mx.append(quantise_piece(n))

from contextlib import ExitStack

import concourse.mybir as mybir
from concourse.masks import make_identity

F32 = mybir.dt.float32
BF16 = mybir.dt.bfloat16
U32 = mybir.dt.uint32
U8 = mybir.dt.uint8
FP8X4 = mybir.dt.float8_e4m3fn_x4
ADD = mybir.AluOpType.add
MULT = mybir.AluOpType.mult
TANH = mybir.ActivationFunctionType.Tanh

P = 128
PACK = 4
B, H, K, O, I = 128, 512, 512, 32, 32
OI = O * I
N_TILE = 512
N_TILES = OI // N_TILE
PSUM_RUN = 2
RUN = 4

FLOPS = 2 * B * H * K + 2 * B * K * OI

V_Q = 64
PIECE = 256
PIECES = OI // PIECE
S_COLS = 128
V_COLS = 192


def regroup(engine_copy, grouped, raw, cols):
    engine_copy(
        out=grouped[:, cols, :].rearrange("p (c i) j -> p c j i", i=RUN),
        in_=raw[:, :, cols].rearrange("p j (c i) -> p c j i", i=RUN),
    )


def tile_structuredternaryfactorgenerator_pa_s_kernel(
    tc, hk, kw2, kb2, bases, base, row, col, weight, coeff
):
    nc = tc.nc
    with ExitStack() as ctx:
        keep = ctx.enter_context(tc.tile_pool(name="keep", bufs=1))
        psum = ctx.enter_context(tc.psum_pool(name="psum", bufs=1))
        ctx.enter_context(tc.manual_schedule())

        def quantise(name, grouped_flat, width):
            codes = keep.tile([P, width], U32, align_bytes=64, name=name + "_codes")
            scales = keep.tile([P, width], U8, align_bytes=64, name=name + "_scales")
            nc.vector.quantize_mx(out=codes[:].bitcast(FP8X4), scales=scales[:], in_=grouped_flat)
            return codes, scales

        def quantise_piece(n):
            first = n * PIECE % N_TILE
            grouped = bases_grouped[n * PIECE // N_TILE][:, first : first + PIECE, :]
            return quantise("bases_piece%d" % n, grouped.rearrange("p c j -> p (c j)"), PIECE)

        row_sb = keep.tile([P, O], BF16)
        nc.sync.dma_start(out=row_sb[:], in_=row)
        col_sb = keep.tile([P, I], BF16)
        nc.sync.dma_start(out=col_sb[:], in_=col)
        hk_sb = keep.tile([P, H], BF16)
        nc.sync.dma_start(out=hk_sb[:], in_=hk)
        kw2_raw = keep.tile([P, PACK, K], BF16)
        nc.sync.dma_start(out=kw2_raw[:], in_=kw2.rearrange("(p j) k -> p j k", j=PACK))
        base_sb = keep.tile([P, 8], BF16)
        nc.sync.dma_start(out=base_sb[:], in_=base.rearrange("o (g e) -> (o g) e", e=8))
        bases_rows = bases.rearrange("(p j) o i -> p j (o i)", j=PACK)
        bases_raw = []
        for n in range(N_TILES):
            raw = keep.tile([P, PACK, N_TILE], BF16, name="bases_raw%d" % n)
            nc.sync.dma_start(out=raw[:], in_=bases_rows[:, :, n * N_TILE : (n + 1) * N_TILE])
            bases_raw.append(raw)
            if n == 0:
                kb2_sb = keep.tile([P, PACK], BF16)
                nc.sync.dma_start(out=kb2_sb[:], in_=kb2.rearrange("(q s) -> q s", s=PACK))

        ident = keep.tile([P, P], F32)
        make_identity(nc, ident[:])
        warm = keep.tile([P, 1], F32)
        nc.vector.memset(warm[:], 0.0)
        nc.scalar.activation(out=warm[:], in_=warm[:], func=TANH)

        gains = keep.tile([P, O, I], F32)
        nc.vector.tensor_tensor(
            out=gains[:],
            in0=row_sb[:].unsqueeze(2).to_broadcast([P, O, I]),
            in1=col_sb[:].unsqueeze(1).to_broadcast([P, O, I]),
            op=MULT,
        )
        gains_flat = gains[:].rearrange("b o i -> b (o i)")


        hk_words = hk_sb[:].bitcast(F32).rearrange("b (p u) -> b u p", u=2)
        hkT_ps = psum.tile([P, 2, B], F32)
        for u in range(2):
            nc.tensor.transpose(hkT_ps[:, u, :], hk_words[:, u, :], ident[:])
        hk_grouped = keep.tile([P, B * PACK], BF16, align_bytes=64)
        nc.vector.tensor_copy(
            out=hk_grouped[:].bitcast(F32).rearrange("p (a i u) -> p a u i", i=PSUM_RUN, u=2),
            in_=hkT_ps[:].rearrange("p u (a i) -> p a u i", i=PSUM_RUN),
        )

        kw2_grouped = keep.tile([P, PACK, P * PACK], BF16, align_bytes=64)
        kw2_dst = kw2_grouped[:].rearrange("p s (c i j) -> p s c j i", i=RUN, j=PACK)
        kw2_src = kw2_raw[:].rearrange("p j (c i s) -> p s c j i", i=RUN, s=PACK)
        nc.vector.tensor_copy(out=kw2_dst[:, 0:2], in_=kw2_src[:, 0:2])
        nc.scalar.copy(out=kw2_dst[:, 3], in_=kw2_src[:, 3])
        nc.scalar.copy(out=kw2_dst[:, 2, V_Q // RUN :], in_=kw2_src[:, 2, V_Q // RUN :])
        nc.vector.tensor_copy(out=kw2_dst[:, 2, 0 : V_Q // RUN], in_=kw2_src[:, 2, 0 : V_Q // RUN])
        hk_codes, hk_scales = quantise("hk", hk_grouped[:], B)

        base_words = base_sb[:].bitcast(F32)
        base_ps = psum.tile([P, 4, P], F32)
        for m in range(4):
            nc.tensor.transpose(base_ps[:, m, :], base_words[:, m : m + 1].to_broadcast([P, P]), ident[:])

        bases_grouped = []
        for n in range(N_TILES):
            grouped = keep.tile([P, N_TILE, PACK], BF16, align_bytes=64, name="bases_grouped%d" % n)
            bases_grouped.append(grouped)
        regroup(nc.scalar.copy, bases_grouped[0], bases_raw[0], slice(0, S_COLS))

        kw2_mx = [quantise("kw2_0", kw2_grouped[:, 0:2, :].rearrange("p s c -> p (s c)"), 2 * P)]
        kw2_mx.append(quantise("kw2_1", kw2_grouped[:, 2:4, :].rearrange("p s c -> p (s c)"), 2 * P))
        coeffT = keep.tile([P, PACK, B], F32)
        for pair in range(2):
            codes, scales = kw2_mx[pair]
            z_ps = []
            for e in range(2):
                z_ps.append(psum.tile([P, B], F32, name="bank%d" % (2 * pair + e)))
                nc.tensor.matmul_mx(
                    out=z_ps[e][:],
                    lhsT=codes[:, e * P : (e + 1) * P].bitcast(FP8X4),
                    lhsT_scale=scales[:, e * P : (e + 1) * P],
                    rhs=hk_codes[:].bitcast(FP8X4),
                    rhs_scale=hk_scales[:],
                    start=True,
                    stop=True,
                )
            for e in range(2):
                s = 2 * pair + e
                nc.scalar.activation(
                    out=coeffT[:, s, :], in_=z_ps[e][:], func=TANH, bias=kb2_sb[:, s : s + 1], scale=1.0
                )

        regroup(nc.vector.tensor_copy, bases_grouped[0], bases_raw[0], slice(S_COLS, PIECE))
        regroup(nc.vector.tensor_copy, bases_grouped[0], bases_raw[0], slice(PIECE, N_TILE))
        regroup(nc.scalar.copy, bases_grouped[1], bases_raw[1], slice(V_COLS, PIECE))
        regroup(nc.scalar.copy, bases_grouped[1], bases_raw[1], slice(PIECE, N_TILE))

        base_all = keep.tile([P, OI], BF16)
        base_dst = base_all[:].bitcast(F32).rearrange("c (a i m) -> c a m i", i=PSUM_RUN, m=4)
        base_src = base_ps[:].rearrange("c m (a i) -> c a m i", i=PSUM_RUN)
        half = P // PSUM_RUN // 2
        for rows in (slice(0, half), slice(half, 2 * half)):
            nc.scalar.copy(out=base_dst[:, rows], in_=base_src[:, rows])

        coeff_grouped = keep.tile([P, B, PACK], BF16, align_bytes=64)
        bases_mx = [quantise_piece(0)]
        regroup(nc.vector.tensor_copy, coeff_grouped, coeffT, slice(0, B))
        regroup(nc.vector.tensor_copy, bases_grouped[1], bases_raw[1], slice(0, V_COLS))
        coeff_codes, coeff_scales = quantise("coeff", coeff_grouped[:].rearrange("q b s -> q (b s)"), B)
        for n in range(1, PIECES):
            bases_mx.append(quantise_piece(n))

        coeff_ps = psum.tile([P, PACK, P], F32)
        for s in range(PACK):
            nc.tensor.transpose(coeff_ps[:, s, :], coeffT[:, s, :], ident[:])
        coeff_sb = keep.tile([P, K], F32)
        nc.scalar.copy(
            out=coeff_sb[:].rearrange("b (a i s) -> b a s i", i=PSUM_RUN, s=PACK),
            in_=coeff_ps[:].rearrange("b s (a i) -> b a s i", i=PSUM_RUN),
        )
        nc.scalar.dma_start(out=coeff, in_=coeff_sb[:])

        weight_flat = weight.rearrange("b o i -> b (o i)")
        summed = keep.tile([P, OI], F32)
        delta_ps = []
        for n in range(PIECES):
            codes, scales = bases_mx[n]
            acc = psum.tile([P, PIECE], F32, name="bank%d" % n)
            delta_ps.append(acc)
            nc.tensor.matmul_mx(
                out=acc[:],
                lhsT=coeff_codes[:].bitcast(FP8X4),
                lhsT_scale=coeff_scales[:],
                rhs=codes[:].bitcast(FP8X4),
                rhs_scale=scales[:],
                start=True,
                stop=True,
            )

        def add_base(n):
            cols = slice(n * PIECE, (n + 1) * PIECE)
            nc.vector.tensor_tensor(out=summed[:, cols], in0=delta_ps[n][:], in1=base_all[:, cols], op=ADD)

        def scale_and_store(n):
            cols = slice(n * PIECE, (n + 1) * PIECE)
            weight_sb = keep.tile([P, PIECE], F32, name="weight_sb%d" % n)
            nc.vector.tensor_tensor(out=weight_sb[:], in0=summed[:, cols], in1=gains_flat[:, cols], op=MULT)
            nc.sync.dma_start(out=weight_flat[:, cols], in_=weight_sb[:])

        add_base(0)
        for n in range(1, PIECES):
            add_base(n)
            scale_and_store(n - 1)
        scale_and_store(PIECES - 1)
